import numpy as np
import ml_dtypes


def mxq(x, axis, fmt="e4m3"):
    dtype, down = {"e4m3": (ml_dtypes.float8_e4m3fn, 7), "e5m2": (ml_dtypes.float8_e5m2, 14)}[fmt]
    v = np.moveaxis(np.asarray(x, np.float32).astype(ml_dtypes.bfloat16).astype(np.float64), axis, -1)
    blocks = v.reshape(v.shape[:-1] + (-1, 32))
    amax = np.abs(blocks).max(-1, keepdims=True)
    byte = np.maximum(np.where(amax > 0, np.frexp(amax)[1] - 1 + 127, 0) - down, 1)
    scale = np.exp2(byte - 127.0)
    codes = (blocks / scale).astype(np.float32).astype(dtype).astype(np.float64)
    return np.moveaxis((codes * scale).reshape(v.shape), -1, axis)


WIDE = False


def mx_kscale(k):
    if not WIDE:
        return np.ones(k)
    levels = np.array([10, -10, 5, -5, 0])
    if k % 512:
        return np.exp2(np.random.permutation(np.resize(levels, k // 32))).repeat(32)
    a = np.empty((k // 512, 16))
    for p in range(k // 512):
        a[p, :8] = np.random.permutation(np.resize(levels, 8))
        for g in range(8):
            far = levels[np.abs(levels - a[p, g]) >= 10]
            a[p, g + 8] = far[np.random.randint(len(far))]
    return np.exp2(a.ravel()).repeat(32)


BF16 = ml_dtypes.bfloat16


def bf(x):
    return np.asarray(x, np.float32).astype(BF16)


def f64(x):
    return np.asarray(x).astype(np.float64)


L, N, E, H, C, LW, RW = 2048, 1, 1024, 8, 512, 1, 1
EPS = 1e-8


def sigmoid(v):
    return 1.0 / (1.0 + np.exp(-v))


def setup_inputs():
    s = mx_kscale(E)
    return {"attn_out": bf(np.random.standard_normal((L, N, E)) * 2.0),
            "norm_scale": bf((1.0 + 0.1 * np.random.standard_normal(E)) * s),
            "norm_gate": bf(1.0 + 0.2 * np.random.standard_normal(E)),
            "w_o": bf(np.random.standard_normal((E, E)) / np.sqrt(E) / s[None, :]),
            "b_o": bf(np.random.standard_normal(E) * 0.1)}


def reference(attn_out, norm_scale, norm_gate, w_o, b_o):
    x = f64(attn_out)
    rms = np.sqrt(np.mean(x * x, axis=-1, keepdims=True))
    y = f64(norm_scale) * (x / (rms + EPS)) * sigmoid(f64(norm_gate) * x)
    return (mxq(y, 2, "e4m3") @ mxq(f64(w_o), 1, "e4m3").T) + f64(b_o)

@@ -1,0 +1,232 @@
+from contextlib import ExitStack
+
+import concourse.mybir as mybir
+from concourse.masks import make_identity
+
+F32 = mybir.dt.float32
+BF16 = mybir.dt.bfloat16
+U32 = mybir.dt.uint32
+U8 = mybir.dt.uint8
+FP8X4 = mybir.dt.float8_e4m3fn_x4
+ACT = mybir.ActivationFunctionType
+ALU = mybir.AluOpType
+
+P = 128
+TOKENS = 2048
+FEAT = 1024
+OUTF = 1024
+EPS = 1e-8
+PACK = 4
+K_PASS = P * PACK
+PASSES = FEAT // K_PASS
+PAIR = 2
+WORD_COLS = FEAT // (PAIR * P)
+PLANES = FEAT // P
+BANK = 512
+GROUP_TILES = 4
+GROUP = GROUP_TILES * P
+GROUPS = TOKENS // GROUP
+OUT_HALVES = OUTF // BANK
+GPSIMD_TOKENS = 256
+
+FLOPS = 2 * TOKENS * FEAT * OUTF
+
+
+def tile_normlocalattention_pb_kernel(tc, attn_out, norm_scale, norm_gate, w_o, b_o, out):
+    nc = tc.nc
+    x_rows = attn_out.rearrange("l n e -> (l n) e")
+    out_rows = out.rearrange("l n f -> (l n) f")
+
+    with ExitStack() as stack:
+        keep = stack.enter_context(tc.tile_pool(name="keep", bufs=1))
+        planes = stack.enter_context(tc.tile_pool(name="planes", bufs=2))
+        small = stack.enter_context(tc.tile_pool(name="small", bufs=2))
+        scratch = stack.enter_context(tc.tile_pool(name="scratch", bufs=4))
+        results = stack.enter_context(tc.tile_pool(name="results", bufs=4))
+        flipped = stack.enter_context(tc.psum_pool(name="flipped", bufs=3))
+        spread = stack.enter_context(tc.psum_pool(name="spread", bufs=1))
+        sums = stack.enter_context(tc.psum_pool(name="sums", bufs=4))
+
+        ident = keep.tile([P, P], F32)
+        make_identity(nc, ident[:])
+        ones = keep.tile([P, P], BF16)
+        nc.vector.memset(ones[:], 1.0)
+        halves_exp = keep.tile([P, GROUP_TILES], F32)
+        nc.vector.memset(halves_exp[:], 0.5)
+        gate_raw = keep.tile([P, PASSES, PACK], BF16)
+        scale_raw = keep.tile([P, PASSES, PACK], BF16)
+        bias_row = keep.tile([P, OUTF], BF16)
+        nc.vector.memset(bias_row[:], 0.0)
+
+        nc.scalar.dma_start(out=gate_raw[:], in_=norm_gate.rearrange("(g p t) -> p g t", g=PASSES, t=PACK))
+        nc.scalar.dma_start(out=scale_raw[:], in_=norm_scale.rearrange("(g p t) -> p g t", g=PASSES, t=PACK))
+        nc.scalar.dma_start(out=bias_row[0:1, :], in_=b_o.rearrange("(r c) -> r c", r=1))
+
+        x_tiles = [keep.tile([P, FEAT], BF16, name="x%d" % i) for i in range(TOKENS // P)]
+        w_tiles = [keep.tile([P, FEAT], BF16, name="w%d" % i) for i in range(OUTF // P)]
+
+        def load_x(i):
+            nc.sync.dma_start(out=x_tiles[i][:], in_=x_rows[i * P : (i + 1) * P, :])
+
+        for i in range(GROUP_TILES):
+            load_x(i)
+        for i in range(OUTF // P):
+            nc.sync.dma_start(out=w_tiles[i][:], in_=w_o[i * P : (i + 1) * P, :])
+        for i in range(GROUP_TILES, TOKENS // P):
+            load_x(i)
+
+        gain_cols = keep.tile([P, 2 * PLANES], F32)
+        nc.vector.tensor_copy(out=gain_cols[:, 0:PLANES], in_=gate_raw[:].rearrange("p g t -> p (g t)"))
+        nc.vector.tensor_copy(out=gain_cols[:, PLANES : 2 * PLANES], in_=scale_raw[:].rearrange("p g t -> p (g t)"))
+
+        def gate_col(c):
+            return gain_cols[:, c : c + 1]
+
+        def scale_col(c):
+            return gain_cols[:, PLANES + c : PLANES + c + 1]
+
+        bias = keep.tile([P, OUTF], F32)
+        for h in range(OUT_HALVES):
+            cols = slice(h * BANK, (h + 1) * BANK)
+            bias_ps = sums.tile([P, BANK], F32, tag="sum")
+            nc.tensor.matmul(out=bias_ps[:], lhsT=ones[:], rhs=bias_row[:, cols], start=True, stop=True)
+            nc.vector.tensor_copy(out=bias[:, cols], in_=bias_ps[:])
+
+        def word_slice(wc):
+            g, u = divmod(wc, PAIR)
+            return slice(g * PAIR * P + u, (g + 1) * PAIR * P, PAIR)
+
+        w_codes = keep.tile([P, PASSES, OUTF], U32, align_bytes=64)
+        w_scales = keep.tile([P, PASSES, OUTF], U8, align_bytes=64)
+
+        def prepare_w():
+            for g in range(PASSES):
+                w_grouped = keep.tile([P, OUTF * PACK], BF16, name="w_grouped%d" % g, align_bytes=64)
+                w_words = w_grouped[:].bitcast(F32).rearrange("p (f u) -> p f u", u=PAIR)
+                for fp in range(OUTF // (2 * P)):
+                    w_t = flipped.tile([P, PAIR, 2 * P], F32, tag="flip")
+                    for u in range(PAIR):
+                        word_cols = word_slice(PAIR * g + u)
+                        for o in range(2):
+                            nc.tensor.transpose(
+                                w_t[:, u, o * P : (o + 1) * P],
+                                w_tiles[2 * fp + o][:].bitcast(F32)[:, word_cols],
+                                ident[:],
+                            )
+                    nc.vector.tensor_copy(
+                        out=w_words[:, fp * 2 * P : (fp + 1) * 2 * P, :], in_=w_t[:].rearrange("p u f -> p f u")
+                    )
+                for h in range(OUT_HALVES):
+                    cols = slice(h * BANK, (h + 1) * BANK)
+                    nc.vector.quantize_mx(
+                        out=w_codes[:, g, cols].bitcast(FP8X4),
+                        scales=w_scales[:, g, cols],
+                        in_=w_grouped[:, h * BANK * PACK : (h + 1) * BANK * PACK],
+                    )
+
+        def gate_group(i):
+            sig = planes.tile([P, PLANES, GROUP], F32, name="sig")
+            z = planes.tile([P, PLANES, GROUP], F32, name="z")
+            for wc in range(WORD_COLS):
+                x_t = flipped.tile([P, GROUP], F32, tag="flip")
+                for j in range(GROUP_TILES):
+                    nc.tensor.transpose(
+                        x_t[:, j * P : (j + 1) * P],
+                        x_tiles[i * GROUP_TILES + j][:].bitcast(F32)[:, word_slice(wc)],
+                        ident[:],
+                    )
+                halves = x_t[:].bitcast(BF16).rearrange("p (k e) -> p k e", e=PAIR)
+                for e in range(PAIR):
+                    c = PAIR * wc + e
+                    nc.scalar.activation(out=sig[:, c, :], in_=halves[:, :, e], func=ACT.Sigmoid, scale=gate_col(c))
+                for e in range(PAIR):
+                    c = PAIR * wc + e
+                    nc.vector.scalar_tensor_tensor(
+                        out=z[:, c, :],
+                        in0=halves[:, :, e],
+                        scalar=scale_col(c),
+                        in1=sig[:, c, :],
+                        op0=ALU.mult,
+                        op1=ALU.mult,
+                    )
+            return z
+
+        def inverse_rms(i):
+            mean_sq = small.tile([P, GROUP_TILES], F32, name="mean_sq")
+            for j in range(GROUP_TILES):
+                squares = scratch.tile([P, FEAT], BF16, name="squares")
+                nc.scalar.activation(
+                    out=squares[:],
+                    in_=x_tiles[i * GROUP_TILES + j][:],
+                    func=ACT.Square,
+                    scale=1.0 / 32.0,
+                    accum_out=mean_sq[:, j : j + 1],
+                )
+            rms = small.tile([P, GROUP_TILES], F32, name="rms")
+            nc.gpsimd.tensor_tensor(out=rms[:], in0=mean_sq[:], in1=halves_exp[:], op=ALU.pow)
+            rms_eps = small.tile([P, GROUP_TILES], F32, name="rms_eps")
+            nc.vector.tensor_scalar_add(out=rms_eps[:], in0=rms[:], scalar1=EPS)
+            inv = small.tile([P, GROUP_TILES], F32, name="inv")
+            nc.vector.reciprocal(out=inv[:], in_=rms_eps[:])
+            inv_ps = spread.tile([P, GROUP], F32, name="inv_ps")
+            for j in range(GROUP_TILES):
+                nc.tensor.matmul(
+                    out=inv_ps[:, j * P : (j + 1) * P],
+                    lhsT=inv[:, j : j + 1].to_broadcast([P, P]),
+                    rhs=ident[:],
+                    start=True,
+                    stop=True,
+                )
+            inv_row = small.tile([P, GROUP], F32, name="inv_row")
+            nc.scalar.copy(out=inv_row[:], in_=inv_ps[:])
+            return inv_row
+
+        def finish_group(i, z, inv_row):
+            y_codes = small.tile([P, PASSES, GROUP], U32, name="y_codes", align_bytes=64)
+            y_scales = small.tile([P, PASSES, GROUP], U8, name="y_scales", align_bytes=64)
+            for g in range(PASSES):
+                y_grouped = small.tile([P, GROUP, PACK], BF16, name="y_grouped", align_bytes=64)
+                for engine, first, n in (
+                    (nc.gpsimd, 0, GPSIMD_TOKENS),
+                    (nc.vector, GPSIMD_TOKENS, GROUP - GPSIMD_TOKENS),
+                ):
+                    toks = slice(first, first + n)
+                    engine.tensor_tensor(
+                        out=y_grouped[:, toks, :],
+                        in0=z[:, g * PACK : (g + 1) * PACK, toks].rearrange("p t k -> p k t"),
+                        in1=inv_row[:, toks].unsqueeze(2).to_broadcast([P, n, PACK]),
+                        op=ALU.mult,
+                    )
+                nc.vector.quantize_mx(
+                    out=y_codes[:, g, :].bitcast(FP8X4),
+                    scales=y_scales[:, g, :],
+                    in_=y_grouped[:].rearrange("p k t -> p (k t)"),
+                )
+            for j in range(GROUP_TILES):
+                toks = slice(j * P, (j + 1) * P)
+                res = results.tile([P, OUTF], F32, name="res")
+                for h in range(OUT_HALVES):
+                    cols = slice(h * BANK, (h + 1) * BANK)
+                    acc = sums.tile([P, BANK], F32, tag="sum")
+                    for g in range(PASSES):
+                        nc.tensor.matmul_mx(
+                            out=acc[:],
+                            lhsT=y_codes[:, g, toks].bitcast(FP8X4),
+                            lhsT_scale=y_scales[:, g, toks],
+                            rhs=w_codes[:, g, cols].bitcast(FP8X4),
+                            rhs_scale=w_scales[:, g, cols],
+                            start=(g == 0),
+                            stop=(g == PASSES - 1),
+                        )
+                    nc.vector.tensor_tensor(out=res[:, cols], in0=acc[:], in1=bias[:, cols], op=ALU.add)
+                row0 = (i * GROUP_TILES + j) * P
+                nc.sync.dma_start(out=out_rows[row0 : row0 + P, :], in_=res[:])
+
+        ready = {}
+        for i in range(GROUPS + 1):
+            if i < GROUPS:
+                ready[i] = (gate_group(i), inverse_rms(i))
+            if i == 0:
+                prepare_w()
+            else:
+                finish_group(i - 1, ready[i - 1][0], ready[i - 1][1])

@@ -17,17 +17,16 @@ FEAT = 1024
 OUTF = 1024
 EPS = 1e-8
 PACK = 4
-K_PASS = P * PACK
-PASSES = FEAT // K_PASS
+PASSES = FEAT // (P * PACK)
 PAIR = 2
-WORD_COLS = FEAT // (PAIR * P)
 PLANES = FEAT // P
 BANK = 512
-GROUP_TILES = 4
-GROUP = GROUP_TILES * P
-GROUPS = TOKENS // GROUP
 OUT_HALVES = OUTF // BANK
-GPSIMD_TOKENS = 256
+UNIT = 2
+WIDTH = UNIT * P
+UNITS = TOKENS // WIDTH
+GROUPS = ((0,), (1,), (2, 3), (4, 5), (6, 7))
+SCALAR_OUT = ()
 
 FLOPS = 2 * TOKENS * FEAT * OUTF
 
@@ -39,194 +38,351 @@ def tile_normlocalattention_pb_kernel(tc, attn_out, norm_scale, norm_gate, w_o, 
 
     with ExitStack() as stack:
         keep = stack.enter_context(tc.tile_pool(name="keep", bufs=1))
-        planes = stack.enter_context(tc.tile_pool(name="planes", bufs=2))
-        small = stack.enter_context(tc.tile_pool(name="small", bufs=2))
-        scratch = stack.enter_context(tc.tile_pool(name="scratch", bufs=4))
+        planes = stack.enter_context(tc.tile_pool(name="planes", bufs=3))
+        small = stack.enter_context(tc.tile_pool(name="small", bufs=3))
         results = stack.enter_context(tc.tile_pool(name="results", bufs=4))
         flipped = stack.enter_context(tc.psum_pool(name="flipped", bufs=3))
-        spread = stack.enter_context(tc.psum_pool(name="spread", bufs=1))
-        sums = stack.enter_context(tc.psum_pool(name="sums", bufs=4))
+        spread = stack.enter_context(tc.psum_pool(name="spread", bufs=2))
+        sums = stack.enter_context(tc.psum_pool(name="sums", bufs=3))
+        stack.enter_context(tc.manual_schedule())
 
-        ident = keep.tile([P, P], F32)
-        make_identity(nc, ident[:])
-        ones = keep.tile([P, P], BF16)
-        nc.vector.memset(ones[:], 1.0)
-        halves_exp = keep.tile([P, GROUP_TILES], F32)
-        nc.vector.memset(halves_exp[:], 0.5)
-        gate_raw = keep.tile([P, PASSES, PACK], BF16)
-        scale_raw = keep.tile([P, PASSES, PACK], BF16)
-        bias_row = keep.tile([P, OUTF], BF16)
-        nc.vector.memset(bias_row[:], 0.0)
-
-        nc.scalar.dma_start(out=gate_raw[:], in_=norm_gate.rearrange("(g p t) -> p g t", g=PASSES, t=PACK))
-        nc.scalar.dma_start(out=scale_raw[:], in_=norm_scale.rearrange("(g p t) -> p g t", g=PASSES, t=PACK))
-        nc.scalar.dma_start(out=bias_row[0:1, :], in_=b_o.rearrange("(r c) -> r c", r=1))
+        gate_raw = keep.tile([P, PLANES], BF16)
+        scale_raw = keep.tile([P, PLANES], BF16)
+        for raw, vec in ((gate_raw, norm_gate), (scale_raw, norm_scale)):
+            nc.scalar.dma_start(
+                out=raw[:].rearrange("p (g t) -> p g t", t=PACK),
+                in_=vec.rearrange("(g p t) -> p g t", g=PASSES, t=PACK),
+            )
+        warm = keep.tile([P, 1], F32)
+        nc.vector.memset(warm[:], 0.0)
+        nc.scalar.activation(out=warm[:], in_=warm[:], func=ACT.Silu)
 
         x_tiles = [keep.tile([P, FEAT], BF16, name="x%d" % i) for i in range(TOKENS // P)]
         w_tiles = [keep.tile([P, FEAT], BF16, name="w%d" % i) for i in range(OUTF // P)]
+        bias_row = keep.tile([P, OUTF], BF16)
+        ident = keep.tile([P, P], F32)
+        make_identity(nc, ident[:])
+        nc.gpsimd.memset(bias_row[:], 0.0)
 
-        def load_x(i):
-            nc.sync.dma_start(out=x_tiles[i][:], in_=x_rows[i * P : (i + 1) * P, :])
+        def load_x(first, last):
+            for i in range(first, last):
+                nc.sync.dma_start(out=x_tiles[i][:], in_=x_rows[i * P : (i + 1) * P, :])
 
-        for i in range(GROUP_TILES):
-            load_x(i)
+        load_x(0, 4)
         for i in range(OUTF // P):
             nc.sync.dma_start(out=w_tiles[i][:], in_=w_o[i * P : (i + 1) * P, :])
-        for i in range(GROUP_TILES, TOKENS // P):
-            load_x(i)
+        nc.sync.dma_start(out=bias_row[0:1, :], in_=b_o.rearrange("(r c) -> r c", r=1))
+        load_x(4, TOKENS // P)
 
-        gain_cols = keep.tile([P, 2 * PLANES], F32)
-        nc.vector.tensor_copy(out=gain_cols[:, 0:PLANES], in_=gate_raw[:].rearrange("p g t -> p (g t)"))
-        nc.vector.tensor_copy(out=gain_cols[:, PLANES : 2 * PLANES], in_=scale_raw[:].rearrange("p g t -> p (g t)"))
+        ones = keep.tile([P, P], BF16)
+        nc.vector.memset(ones[:], 1.0)
+        halves_exp = keep.tile([P, 2 * UNIT], F32)
+        nc.vector.memset(halves_exp[:], 0.5)
 
-        def gate_col(c):
-            return gain_cols[:, c : c + 1]
+        gate_abs = keep.tile([P, PLANES], F32)
+        nc.vector.scalar_tensor_tensor(
+            out=gate_abs[:], in0=gate_raw[:], scalar=-1.0, in1=gate_raw[:], op0=ALU.mult, op1=ALU.max
+        )
+        gate_zero = keep.tile([P, PLANES], F32)
+        nc.vector.tensor_scalar(
+            out=gate_zero[:], in0=gate_abs[:], scalar1=1e-20, scalar2=2e-20, op0=ALU.is_lt, op1=ALU.mult
+        )
+        gate = keep.tile([P, PLANES], F32)
+        nc.vector.tensor_tensor(out=gate[:], in0=gate_zero[:], in1=gate_raw[:], op=ALU.add)
+        gate_inv = keep.tile([P, PLANES], F32)
+        nc.vector.reciprocal(out=gate_inv[:], in_=gate[:])
+        ratio = keep.tile([P, PLANES], F32)
+        nc.vector.tensor_tensor(out=ratio[:], in0=gate_inv[:], in1=scale_raw[:], op=ALU.mult)
 
-        def scale_col(c):
-            return gain_cols[:, PLANES + c : PLANES + c + 1]
-
-        bias = keep.tile([P, OUTF], F32)
-        for h in range(OUT_HALVES):
-            cols = slice(h * BANK, (h + 1) * BANK)
-            bias_ps = sums.tile([P, BANK], F32, tag="sum")
-            nc.tensor.matmul(out=bias_ps[:], lhsT=ones[:], rhs=bias_row[:, cols], start=True, stop=True)
-            nc.vector.tensor_copy(out=bias[:, cols], in_=bias_ps[:])
-
-        def word_slice(wc):
-            g, u = divmod(wc, PAIR)
+        def word_slice(g, u):
             return slice(g * PAIR * P + u, (g + 1) * PAIR * P, PAIR)
 
-        w_codes = keep.tile([P, PASSES, OUTF], U32, align_bytes=64)
-        w_scales = keep.tile([P, PASSES, OUTF], U8, align_bytes=64)
+        z, mean_sq, inv, inv_ps, x_flip, y_grouped, y_codes, y_scales, res, acc = ({} for i in range(10))
+        group_of = {k: i for i, units in enumerate(GROUPS) for k in units}
 
-        def prepare_w():
-            for g in range(PASSES):
-                w_grouped = keep.tile([P, OUTF * PACK], BF16, name="w_grouped%d" % g, align_bytes=64)
-                w_words = w_grouped[:].bitcast(F32).rearrange("p (f u) -> p f u", u=PAIR)
-                for fp in range(OUTF // (2 * P)):
-                    w_t = flipped.tile([P, PAIR, 2 * P], F32, tag="flip")
-                    for u in range(PAIR):
-                        word_cols = word_slice(PAIR * g + u)
-                        for o in range(2):
-                            nc.tensor.transpose(
-                                w_t[:, u, o * P : (o + 1) * P],
-                                w_tiles[2 * fp + o][:].bitcast(F32)[:, word_cols],
-                                ident[:],
-                            )
-                    nc.vector.tensor_copy(
-                        out=w_words[:, fp * 2 * P : (fp + 1) * 2 * P, :], in_=w_t[:].rearrange("p u f -> p f u")
-                    )
-                for h in range(OUT_HALVES):
-                    cols = slice(h * BANK, (h + 1) * BANK)
-                    nc.vector.quantize_mx(
-                        out=w_codes[:, g, cols].bitcast(FP8X4),
-                        scales=w_scales[:, g, cols],
-                        in_=w_grouped[:, h * BANK * PACK : (h + 1) * BANK * PACK],
-                    )
+        def tokens_of(i):
+            return len(GROUPS[i]) * WIDTH
 
-        def gate_group(i):
-            sig = planes.tile([P, PLANES, GROUP], F32, name="sig")
-            z = planes.tile([P, PLANES, GROUP], F32, name="z")
-            for wc in range(WORD_COLS):
-                x_t = flipped.tile([P, GROUP], F32, tag="flip")
-                for j in range(GROUP_TILES):
+        def tiles_of(i):
+            return range(UNIT * GROUPS[i][0], UNIT * (GROUPS[i][-1] + 1))
+
+        def toks_of(k):
+            first = (k - GROUPS[group_of[k]][0]) * WIDTH
+            return slice(first, first + WIDTH)
+
+        def flip(i, b):
+            n = tokens_of(i)
+            per_bank = BANK // n
+            x_flip[i, b] = flipped.tile([P, per_bank, n], F32, name="x_flip", tag="flip")
+            for s in range(per_bank):
+                g, u = divmod(b * per_bank + s, PAIR)
+                for j, t in enumerate(tiles_of(i)):
                     nc.tensor.transpose(
-                        x_t[:, j * P : (j + 1) * P],
-                        x_tiles[i * GROUP_TILES + j][:].bitcast(F32)[:, word_slice(wc)],
-                        ident[:],
+                        x_flip[i, b][:, s, j * P : (j + 1) * P], x_tiles[t][:].bitcast(F32)[:, word_slice(g, u)], ident[:]
                     )
-                halves = x_t[:].bitcast(BF16).rearrange("p (k e) -> p k e", e=PAIR)
-                for e in range(PAIR):
-                    c = PAIR * wc + e
-                    nc.scalar.activation(out=sig[:, c, :], in_=halves[:, :, e], func=ACT.Sigmoid, scale=gate_col(c))
-                for e in range(PAIR):
-                    c = PAIR * wc + e
+
+        def planes_of(i, b):
+            per_bank = BANK // tokens_of(i)
+            return range(PAIR * per_bank * b, PAIR * per_bank * (b + 1))
+
+        def silu(i, b):
+            if b == 0:
+                z[i] = planes.tile([P, PLANES, BANK], F32, name="z")
+            n = tokens_of(i)
+            for c in planes_of(i, b):
+                s, e = divmod(c - planes_of(i, b)[0], PAIR)
+                half = x_flip[i, b][:, s, :].bitcast(BF16).rearrange("p (n e) -> p n e", e=PAIR)[:, :, e]
+                nc.scalar.activation(out=z[i][:, c, 0:n], in_=half, func=ACT.Silu, scale=gate[:, c : c + 1])
+
+        def gain(i, b):
+            n = tokens_of(i)
+            for c in planes_of(i, b):
+                nc.gpsimd.tensor_scalar(
+                    out=z[i][:, c, 0:n],
+                    in0=z[i][:, c, 0:n],
+                    scalar1=ratio[:, c : c + 1],
+                    scalar2=0.0,
+                    op0=ALU.mult,
+                    op1=ALU.add,
+                )
+
+        def square(i, on_vector=()):
+            mean_sq[i] = small.tile([P, 2 * UNIT], F32, name="mean_sq")
+            for j, t in enumerate(tiles_of(i)):
+                squares = small.tile([P, FEAT], BF16, name="squares")
+                if t in on_vector:
                     nc.vector.scalar_tensor_tensor(
-                        out=z[:, c, :],
-                        in0=halves[:, :, e],
-                        scalar=scale_col(c),
-                        in1=sig[:, c, :],
+                        out=squares[:],
+                        in0=x_tiles[t][:],
+                        scalar=1.0 / FEAT,
+                        in1=x_tiles[t][:],
                         op0=ALU.mult,
                         op1=ALU.mult,
+                        accum_out=mean_sq[i][:, j : j + 1],
                     )
-            return z
+                else:
+                    nc.scalar.activation(
+                        out=squares[:],
+                        in_=x_tiles[t][:],
+                        func=ACT.Square,
+                        scale=1.0 / 32.0,
+                        accum_out=mean_sq[i][:, j : j + 1],
+                    )
 
-        def inverse_rms(i):
-            mean_sq = small.tile([P, GROUP_TILES], F32, name="mean_sq")
-            for j in range(GROUP_TILES):
-                squares = scratch.tile([P, FEAT], BF16, name="squares")
-                nc.scalar.activation(
-                    out=squares[:],
-                    in_=x_tiles[i * GROUP_TILES + j][:],
-                    func=ACT.Square,
-                    scale=1.0 / 32.0,
-                    accum_out=mean_sq[:, j : j + 1],
-                )
-            rms = small.tile([P, GROUP_TILES], F32, name="rms")
-            nc.gpsimd.tensor_tensor(out=rms[:], in0=mean_sq[:], in1=halves_exp[:], op=ALU.pow)
-            rms_eps = small.tile([P, GROUP_TILES], F32, name="rms_eps")
-            nc.vector.tensor_scalar_add(out=rms_eps[:], in0=rms[:], scalar1=EPS)
-            inv = small.tile([P, GROUP_TILES], F32, name="inv")
-            nc.vector.reciprocal(out=inv[:], in_=rms_eps[:])
-            inv_ps = spread.tile([P, GROUP], F32, name="inv_ps")
-            for j in range(GROUP_TILES):
+        def root(i):
+            m = len(tiles_of(i))
+            inv[i] = small.tile([P, 2 * UNIT], F32, name="inv")
+            nc.gpsimd.tensor_tensor(out=inv[i][:, 0:m], in0=mean_sq[i][:, 0:m], in1=halves_exp[:, 0:m], op=ALU.pow)
+
+        def invert(i):
+            m = len(tiles_of(i))
+            nc.vector.tensor_scalar_add(out=inv[i][:, 0:m], in0=inv[i][:, 0:m], scalar1=EPS)
+            nc.vector.reciprocal(out=inv[i][:, 0:m], in_=inv[i][:, 0:m])
+
+        def spread_inv(i):
+            inv_ps[i] = spread.tile([P, BANK], F32, name="inv_ps")
+            for j in range(len(tiles_of(i))):
                 nc.tensor.matmul(
-                    out=inv_ps[:, j * P : (j + 1) * P],
-                    lhsT=inv[:, j : j + 1].to_broadcast([P, P]),
+                    out=inv_ps[i][:, j * P : (j + 1) * P],
+                    lhsT=inv[i][:, j : j + 1].to_broadcast([P, P]),
                     rhs=ident[:],
                     start=True,
                     stop=True,
                 )
-            inv_row = small.tile([P, GROUP], F32, name="inv_row")
-            nc.scalar.copy(out=inv_row[:], in_=inv_ps[:])
-            return inv_row
 
-        def finish_group(i, z, inv_row):
-            y_codes = small.tile([P, PASSES, GROUP], U32, name="y_codes", align_bytes=64)
-            y_scales = small.tile([P, PASSES, GROUP], U8, name="y_scales", align_bytes=64)
+        def product(k, g):
+            if g == 0:
+                y_grouped[k] = small.tile([P, PASSES, WIDTH, PACK], BF16, name="y_grouped", align_bytes=64)
+            i, toks = group_of[k], toks_of(k)
+            nc.vector.tensor_tensor(
+                out=y_grouped[k][:, g],
+                in0=z[i][:, g * PACK : (g + 1) * PACK, toks].rearrange("p t n -> p n t"),
+                in1=inv_ps[i][:, toks].unsqueeze(2).to_broadcast([P, WIDTH, PACK]),
+                op=ALU.mult,
+            )
+
+        def quantise(k):
+            y_codes[k] = small.tile([P, PASSES, WIDTH], U32, name="y_codes", align_bytes=64)
+            y_scales[k] = small.tile([P, PASSES, WIDTH], U8, name="y_scales", align_bytes=64)
+            nc.vector.quantize_mx(
+                out=y_codes[k][:].rearrange("p g n -> p (g n)").bitcast(FP8X4),
+                scales=y_scales[k][:].rearrange("p g n -> p (g n)"),
+                in_=y_grouped[k][:].rearrange("p g n t -> p (g n t)"),
+            )
+
+        def matmuls(k, j, h):
+            acc[k, j, h] = sums.tile([P, BANK], F32, name="acc", tag="sum")
+            toks = slice(j * P, (j + 1) * P)
+            cols = slice(h * BANK, (h + 1) * BANK)
             for g in range(PASSES):
-                y_grouped = small.tile([P, GROUP, PACK], BF16, name="y_grouped", align_bytes=64)
-                for engine, first, n in (
-                    (nc.gpsimd, 0, GPSIMD_TOKENS),
-                    (nc.vector, GPSIMD_TOKENS, GROUP - GPSIMD_TOKENS),
-                ):
-                    toks = slice(first, first + n)
-                    engine.tensor_tensor(
-                        out=y_grouped[:, toks, :],
-                        in0=z[:, g * PACK : (g + 1) * PACK, toks].rearrange("p t k -> p k t"),
-                        in1=inv_row[:, toks].unsqueeze(2).to_broadcast([P, n, PACK]),
-                        op=ALU.mult,
-                    )
-                nc.vector.quantize_mx(
-                    out=y_codes[:, g, :].bitcast(FP8X4),
-                    scales=y_scales[:, g, :],
-                    in_=y_grouped[:].rearrange("p k t -> p (k t)"),
+                nc.tensor.matmul_mx(
+                    out=acc[k, j, h][:],
+                    lhsT=y_codes[k][:, g, toks].bitcast(FP8X4),
+                    lhsT_scale=y_scales[k][:, g, toks],
+                    rhs=w_codes[:, g, cols].bitcast(FP8X4),
+                    rhs_scale=w_scales[:, g, cols],
+                    start=(g == 0),
+                    stop=(g == PASSES - 1),
                 )
-            for j in range(GROUP_TILES):
-                toks = slice(j * P, (j + 1) * P)
-                res = results.tile([P, OUTF], F32, name="res")
-                for h in range(OUT_HALVES):
-                    cols = slice(h * BANK, (h + 1) * BANK)
-                    acc = sums.tile([P, BANK], F32, tag="sum")
-                    for g in range(PASSES):
-                        nc.tensor.matmul_mx(
-                            out=acc[:],
-                            lhsT=y_codes[:, g, toks].bitcast(FP8X4),
-                            lhsT_scale=y_scales[:, g, toks],
-                            rhs=w_codes[:, g, cols].bitcast(FP8X4),
-                            rhs_scale=w_scales[:, g, cols],
-                            start=(g == 0),
-                            stop=(g == PASSES - 1),
-                        )
-                    nc.vector.tensor_tensor(out=res[:, cols], in0=acc[:], in1=bias[:, cols], op=ALU.add)
-                row0 = (i * GROUP_TILES + j) * P
-                nc.sync.dma_start(out=out_rows[row0 : row0 + P, :], in_=res[:])
 
-        ready = {}
-        for i in range(GROUPS + 1):
-            if i < GROUPS:
-                ready[i] = (gate_group(i), inverse_rms(i))
-            if i == 0:
-                prepare_w()
+        def finish(k, j, h):
+            if h == 0:
+                res[k, j] = results.tile([P, OUTF], F32, name="res")
+            cols = slice(h * BANK, (h + 1) * BANK)
+            if (k, j, h) in SCALAR_OUT:
+                part = results.tile([P, BANK], F32, name="part")
+                nc.scalar.copy(out=part[:], in_=acc[k, j, h][:])
+                nc.gpsimd.tensor_tensor(out=res[k, j][:, cols], in0=part[:], in1=bias[:, cols], op=ALU.add)
             else:
-                finish_group(i - 1, ready[i - 1][0], ready[i - 1][1])
+                nc.vector.tensor_tensor(out=res[k, j][:, cols], in0=acc[k, j, h][:], in1=bias[:, cols], op=ALU.add)
+            row0 = (UNIT * k + j) * P
+            if k == UNITS - 1:
+                nc.sync.dma_start(out=out_rows[row0 : row0 + P, cols], in_=res[k, j][:, cols])
+            elif h == OUT_HALVES - 1:
+                nc.sync.dma_start(out=out_rows[row0 : row0 + P, :], in_=res[k, j][:])
+
+        w_codes = keep.tile([P, PASSES, OUTF], U32, align_bytes=64)
+        w_scales = keep.tile([P, PASSES, OUTF], U8, align_bytes=64)
+        w_grouped = {}
+
+        def group_w(h, engine_copy):
+            for g in range(PASSES):
+                w_grouped[g, h] = keep.tile([P, BANK * PACK], BF16, name="w_grouped%d%d" % (g, h), align_bytes=64)
+                w_words = w_grouped[g, h][:].bitcast(F32).rearrange("p (f u) -> p f u", u=PAIR)
+                for fp in range(2):
+                    w_t = flipped.tile([P, PAIR, 2 * P], F32, name="w_t", tag="flip")
+                    for u in range(PAIR):
+                        for o in range(2):
+                            nc.tensor.transpose(
+                                w_t[:, u, o * P : (o + 1) * P],
+                                w_tiles[4 * h + 2 * fp + o][:].bitcast(F32)[:, word_slice(g, u)],
+                                ident[:],
+                            )
+                    engine_copy(
+                        out=w_words[:, fp * 2 * P : (fp + 1) * 2 * P, :], in_=w_t[:].rearrange("p u f -> p f u")
+                    )
+
+        def quantise_w(h):
+            cols = slice(h * BANK, (h + 1) * BANK)
+            for g in range(PASSES):
+                nc.vector.quantize_mx(
+                    out=w_codes[:, g, cols].bitcast(FP8X4), scales=w_scales[:, g, cols], in_=w_grouped[g, h][:]
+                )
+
+        bias = keep.tile([P, OUTF], F32)
+
+        def spread_bias():
+            for h in range(OUT_HALVES):
+                cols = slice(h * BANK, (h + 1) * BANK)
+                bias_ps = sums.tile([P, BANK], F32, name="bias_ps", tag="sum")
+                nc.tensor.matmul(out=bias_ps[:], lhsT=ones[:], rhs=bias_row[:, cols], start=True, stop=True)
+                nc.scalar.copy(out=bias[:, cols], in_=bias_ps[:])
+
+        tiles = [(j, h) for j in range(UNIT) for h in range(OUT_HALVES)]
+        square(0, on_vector=(0, 1))
+        flip(0, 0)
+        flip(0, 1)
+        silu(0, 0)
+        gain(0, 0)
+        root(0)
+        silu(0, 1)
+        gain(0, 1)
+        square(1)
+        root(1)
+        group_w(0, nc.vector.tensor_copy)
+        invert(0)
+        spread_inv(0)
+        group_w(1, nc.scalar.copy)
+        flip(1, 0)
+        flip(1, 1)
+        spread_bias()
+        silu(1, 0)
+        gain(1, 0)
+        silu(1, 1)
+        gain(1, 1)
+        product(0, 0)
+        product(0, 1)
+        quantise_w(0)
+        quantise(0)
+        invert(1)
+        quantise_w(1)
+        spread_inv(1)
+        for t in tiles[:3]:
+            matmuls(0, *t)
+
+        flip(2, 0)
+        square(2)
+        root(2)
+        flip(2, 1)
+        product(1, 0)
+        finish(0, *tiles[0])
+        matmuls(0, *tiles[3])
+        flip(2, 2)
+        silu(2, 0)
+        gain(2, 0)
+        silu(2, 1)
+        gain(2, 1)
+        product(1, 1)
+        finish(0, *tiles[1])
+        quantise(1)
+        finish(0, *tiles[2])
+        invert(2)
+        finish(0, *tiles[3])
+        for t in tiles[:3]:
+            matmuls(1, *t)
+        spread_inv(2)
+        flip(2, 3)
+        silu(2, 2)
+        gain(2, 2)
+        silu(2, 3)
+        gain(2, 3)
+
+        for i in range(2, len(GROUPS)):
+            a, b = GROUPS[i]
+            more = i + 1 < len(GROUPS)
+            if more:
+                square(i + 1)
+                root(i + 1)
+            product(a, 0)
+            finish(a - 1, *tiles[0])
+            matmuls(a - 1, *tiles[3])
+            if more:
+                flip(i + 1, 0)
+                flip(i + 1, 1)
+                silu(i + 1, 0)
+                gain(i + 1, 0)
+            product(b, 0)
+            finish(a - 1, *tiles[1])
+            product(a, 1)
+            finish(a - 1, *tiles[2])
+            quantise(a)
+            finish(a - 1, *tiles[3])
+            for t in tiles[:3]:
+                matmuls(a, *t)
+            if more:
+                flip(i + 1, 2)
+                silu(i + 1, 1)
+                gain(i + 1, 1)
+                invert(i + 1)
+                spread_inv(i + 1)
+            product(b, 1)
+            finish(a, *tiles[0])
+            matmuls(a, *tiles[3])
+            finish(a, *tiles[1])
+            quantise(b)
+            finish(a, *tiles[2])
+            if more:
+                flip(i + 1, 3)
+                silu(i + 1, 2)
+                gain(i + 1, 2)
+            finish(a, *tiles[3])
+            for t in tiles[:3]:
+                matmuls(b, *t)
+            if more:
+                silu(i + 1, 3)
+                gain(i + 1, 3)
+        last = UNITS - 1
+        finish(last, *tiles[0])
+        matmuls(last, *tiles[3])
+        for t in tiles[1:]:
+            finish(last, *t)

@@ -195,9 +195,12 @@ def tile_normlocalattention_pb_kernel(tc, attn_out, norm_scale, norm_gate, w_o, 
                 y_grouped[k] = small.tile([P, PASSES, WIDTH, PACK], BF16, name="y_grouped", align_bytes=64)
             i, toks = group_of[k], toks_of(k)
             nc.vector.tensor_tensor(
-                out=y_grouped[k][:, g],
-                in0=z[i][:, g * PACK : (g + 1) * PACK, toks].rearrange("p t n -> p n t"),
-                in1=inv_ps[i][:, toks].unsqueeze(2).to_broadcast([P, WIDTH, PACK]),
+                out=y_grouped[k][:, g].rearrange("p (c i) t -> p c t i", i=PACK),
+                in0=z[i][:, g * PACK : (g + 1) * PACK, toks].rearrange("p t (c i) -> p c t i", i=PACK),
+                in1=inv_ps[i][:, toks]
+                .rearrange("p (c i) -> p c i", i=PACK)
+                .unsqueeze(2)
+                .to_broadcast([P, WIDTH // PACK, PACK, PACK]),
                 op=ALU.mult,
             )
 

@@ -248,22 +248,19 @@ def tile_normlocalattention_pb_kernel(tc, attn_out, norm_scale, norm_gate, w_o, 
         w_scales = keep.tile([P, PASSES, OUTF], U8, align_bytes=64)
         w_grouped = {}
 
-        def group_w(h, engine_copy):
-            for g in range(PASSES):
+        def group_w(h, g, fp, engine_copy):
+            if fp == 0:
                 w_grouped[g, h] = keep.tile([P, BANK * PACK], BF16, name="w_grouped%d%d" % (g, h), align_bytes=64)
-                w_words = w_grouped[g, h][:].bitcast(F32).rearrange("p (f u) -> p f u", u=PAIR)
-                for fp in range(2):
-                    w_t = flipped.tile([P, PAIR, 2 * P], F32, name="w_t", tag="flip")
-                    for u in range(PAIR):
-                        for o in range(2):
-                            nc.tensor.transpose(
-                                w_t[:, u, o * P : (o + 1) * P],
-                                w_tiles[4 * h + 2 * fp + o][:].bitcast(F32)[:, word_slice(g, u)],
-                                ident[:],
-                            )
-                    engine_copy(
-                        out=w_words[:, fp * 2 * P : (fp + 1) * 2 * P, :], in_=w_t[:].rearrange("p u f -> p f u")
+            w_words = w_grouped[g, h][:].bitcast(F32).rearrange("p (f u) -> p f u", u=PAIR)
+            w_t = flipped.tile([P, PAIR, 2 * P], F32, name="w_t", tag="flip")
+            for u in range(PAIR):
+                for o in range(2):
+                    nc.tensor.transpose(
+                        w_t[:, u, o * P : (o + 1) * P],
+                        w_tiles[4 * h + 2 * fp + o][:].bitcast(F32)[:, word_slice(g, u)],
+                        ident[:],
                     )
+            engine_copy(out=w_words[:, fp * 2 * P : (fp + 1) * 2 * P, :], in_=w_t[:].rearrange("p u f -> p f u"))
 
         def quantise_w(h):
             cols = slice(h * BANK, (h + 1) * BANK)
@@ -290,100 +287,70 @@ def tile_normlocalattention_pb_kernel(tc, attn_out, norm_scale, norm_gate, w_o, 
         root(0)
         silu(0, 1)
         gain(0, 1)
-        square(1)
-        root(1)
-        group_w(0, nc.vector.tensor_copy)
+        for g in range(PASSES):
+            for fp in range(2):
+                group_w(0, g, fp, nc.scalar.copy)
+        square(1, on_vector=(2, 3))
         invert(0)
-        spread_inv(0)
-        group_w(1, nc.scalar.copy)
+        root(1)
         flip(1, 0)
         flip(1, 1)
-        spread_bias()
         silu(1, 0)
         gain(1, 0)
         silu(1, 1)
         gain(1, 1)
+        spread_inv(0)
         product(0, 0)
         product(0, 1)
+        for g in range(PASSES):
+            for fp in range(2):
+                group_w(1, g, fp, nc.scalar.copy)
+        invert(1)
+        spread_bias()
+        spread_inv(1)
         quantise_w(0)
         quantise(0)
-        invert(1)
         quantise_w(1)
-        spread_inv(1)
+        flip(2, 0)
         for t in tiles[:3]:
             matmuls(0, *t)
 
-        flip(2, 0)
-        square(2)
-        root(2)
-        flip(2, 1)
-        product(1, 0)
-        finish(0, *tiles[0])
-        matmuls(0, *tiles[3])
-        flip(2, 2)
-        silu(2, 0)
-        gain(2, 0)
-        silu(2, 1)
-        gain(2, 1)
-        product(1, 1)
-        finish(0, *tiles[1])
-        quantise(1)
-        finish(0, *tiles[2])
-        invert(2)
-        finish(0, *tiles[3])
-        for t in tiles[:3]:
-            matmuls(1, *t)
-        spread_inv(2)
-        flip(2, 3)
-        silu(2, 2)
-        gain(2, 2)
-        silu(2, 3)
-        gain(2, 3)
-
-        for i in range(2, len(GROUPS)):
-            a, b = GROUPS[i]
+        for k in range(1, UNITS):
+            i = group_of[k]
+            begins, ends = k == GROUPS[i][0], k == GROUPS[i][-1]
             more = i + 1 < len(GROUPS)
-            if more:
+            if more and begins:
                 square(i + 1)
                 root(i + 1)
-            product(a, 0)
-            finish(a - 1, *tiles[0])
-            matmuls(a - 1, *tiles[3])
-            if more:
-                flip(i + 1, 0)
+            product(k, 0)
+            finish(k - 1, *tiles[0])
+            matmuls(k - 1, *tiles[3])
+            if more and begins:
+                if k > 1:
+                    flip(i + 1, 0)
                 flip(i + 1, 1)
+                flip(i + 1, 2)
                 silu(i + 1, 0)
                 gain(i + 1, 0)
-            product(b, 0)
-            finish(a - 1, *tiles[1])
-            product(a, 1)
-            finish(a - 1, *tiles[2])
-            quantise(a)
-            finish(a - 1, *tiles[3])
-            for t in tiles[:3]:
-                matmuls(a, *t)
-            if more:
-                flip(i + 1, 2)
+            product(k, 1)
+            finish(k - 1, *tiles[1])
+            if more and ends:
+                flip(i + 1, 3)
                 silu(i + 1, 1)
                 gain(i + 1, 1)
+            quantise(k)
+            finish(k - 1, *tiles[2])
+            if more and ends:
                 invert(i + 1)
                 spread_inv(i + 1)
-            product(b, 1)
-            finish(a, *tiles[0])
-            matmuls(a, *tiles[3])
-            finish(a, *tiles[1])
-            quantise(b)
-            finish(a, *tiles[2])
-            if more:
-                flip(i + 1, 3)
+            for t in tiles[:3]:
+                matmuls(k, *t)
+            if more and ends:
                 silu(i + 1, 2)
                 gain(i + 1, 2)
-            finish(a, *tiles[3])
-            for t in tiles[:3]:
-                matmuls(b, *t)
-            if more:
                 silu(i + 1, 3)
                 gain(i + 1, 3)
+            finish(k - 1, *tiles[3])
         last = UNITS - 1
         finish(last, *tiles[0])
         matmuls(last, *tiles[3])

@@ -182,16 +182,12 @@ def tile_normlocalattention_pb_kernel(tc, attn_out, norm_scale, norm_gate, w_o, 
         def spread_inv(i):
             inv_ps[i] = spread.tile([P, BANK], F32, name="inv_ps")
             for j in range(len(tiles_of(i))):
-                nc.tensor.matmul(
-                    out=inv_ps[i][:, j * P : (j + 1) * P],
-                    lhsT=inv[i][:, j : j + 1].to_broadcast([P, P]),
-                    rhs=ident[:],
-                    start=True,
-                    stop=True,
+                nc.tensor.transpose(
+                    inv_ps[i][:, j * P : (j + 1) * P], inv[i][:, j : j + 1].to_broadcast([P, P]), ident[:]
                 )
 
         def product(k, g):
-            if g == 0:
+            if k not in y_grouped:
                 y_grouped[k] = small.tile([P, PASSES, WIDTH, PACK], BF16, name="y_grouped", align_bytes=64)
             i, toks = group_of[k], toks_of(k)
             nc.vector.tensor_tensor(

@@ -41,8 +41,8 @@ def tile_normlocalattention_pb_kernel(tc, attn_out, norm_scale, norm_gate, w_o, 
         planes = stack.enter_context(tc.tile_pool(name="planes", bufs=3))
         small = stack.enter_context(tc.tile_pool(name="small", bufs=3))
         results = stack.enter_context(tc.tile_pool(name="results", bufs=4))
-        flipped = stack.enter_context(tc.psum_pool(name="flipped", bufs=3))
-        spread = stack.enter_context(tc.psum_pool(name="spread", bufs=2))
+        flipped = stack.enter_context(tc.psum_pool(name="flipped", bufs=4))
+        spread = stack.enter_context(tc.psum_pool(name="spread", bufs=1))
         sums = stack.enter_context(tc.psum_pool(name="sums", bufs=3))
         stack.enter_context(tc.manual_schedule())
 
@@ -76,6 +76,13 @@ def tile_normlocalattention_pb_kernel(tc, attn_out, norm_scale, norm_gate, w_o, 
 
         ones = keep.tile([P, P], BF16)
         nc.vector.memset(ones[:], 1.0)
+        warm_in = keep.tile([P, P], F32)
+        nc.vector.memset(warm_in[:], 0.0)
+        warm_ps = sums.tile([P, P], F32, name="warm_ps", tag="sum")
+
+        def keep_warm(n):
+            for r in range(n):
+                nc.tensor.matmul(out=warm_ps[:], lhsT=warm_in[:], rhs=warm_in[:], start=True, stop=True)
         halves_exp = keep.tile([P, 2 * UNIT], F32)
         nc.vector.memset(halves_exp[:], 0.5)
 
@@ -267,27 +274,23 @@ def tile_normlocalattention_pb_kernel(tc, attn_out, norm_scale, norm_gate, w_o, 
 
         bias = keep.tile([P, OUTF], F32)
 
-        def spread_bias():
+        def spread_bias(engine_copy):
             for h in range(OUT_HALVES):
                 cols = slice(h * BANK, (h + 1) * BANK)
                 bias_ps = sums.tile([P, BANK], F32, name="bias_ps", tag="sum")
                 nc.tensor.matmul(out=bias_ps[:], lhsT=ones[:], rhs=bias_row[:, cols], start=True, stop=True)
-                nc.scalar.copy(out=bias[:, cols], in_=bias_ps[:])
+                engine_copy(out=bias[:, cols], in_=bias_ps[:])
 
         tiles = [(j, h) for j in range(UNIT) for h in range(OUT_HALVES)]
         square(0, on_vector=(0, 1))
+        root(0)
         flip(0, 0)
         flip(0, 1)
         silu(0, 0)
         gain(0, 0)
-        root(0)
         silu(0, 1)
         gain(0, 1)
-        for g in range(PASSES):
-            for fp in range(2):
-                group_w(0, g, fp, nc.scalar.copy)
         square(1, on_vector=(2, 3))
-        invert(0)
         root(1)
         flip(1, 0)
         flip(1, 1)
@@ -295,23 +298,52 @@ def tile_normlocalattention_pb_kernel(tc, attn_out, norm_scale, norm_gate, w_o, 
         gain(1, 0)
         silu(1, 1)
         gain(1, 1)
+        invert(0)
+        for g in range(PASSES):
+            for fp in range(2):
+                group_w(0, g, fp, nc.vector.tensor_copy)
         spread_inv(0)
-        product(0, 0)
-        product(0, 1)
+        square(2)
+        root(2)
         for g in range(PASSES):
             for fp in range(2):
                 group_w(1, g, fp, nc.scalar.copy)
+        product(0, 0)
+        product(0, 1)
         invert(1)
-        spread_bias()
+        spread_bias(nc.scalar.copy)
         spread_inv(1)
         quantise_w(0)
         quantise(0)
-        quantise_w(1)
         flip(2, 0)
+        flip(2, 1)
+        silu(2, 0)
+        gain(2, 0)
+        silu(2, 1)
+        gain(2, 1)
+        quantise_w(1)
+        product(1, 0)
         for t in tiles[:3]:
             matmuls(0, *t)
+        finish(0, *tiles[0])
+        matmuls(0, *tiles[3])
+        flip(2, 2)
+        flip(2, 3)
+        silu(2, 2)
+        gain(2, 2)
+        silu(2, 3)
+        gain(2, 3)
+        product(1, 1)
+        finish(0, *tiles[1])
+        invert(2)
+        quantise(1)
+        finish(0, *tiles[2])
+        spread_inv(2)
+        for t in tiles[:3]:
+            matmuls(1, *t)
+        finish(0, *tiles[3])
 
-        for k in range(1, UNITS):
+        for k in range(2, UNITS):
             i = group_of[k]
             begins, ends = k == GROUPS[i][0], k == GROUPS[i][-1]
             more = i + 1 < len(GROUPS)
@@ -322,30 +354,25 @@ def tile_normlocalattention_pb_kernel(tc, attn_out, norm_scale, norm_gate, w_o, 
             finish(k - 1, *tiles[0])
             matmuls(k - 1, *tiles[3])
             if more and begins:
-                if k > 1:
-                    flip(i + 1, 0)
-                flip(i + 1, 1)
-                flip(i + 1, 2)
-                silu(i + 1, 0)
-                gain(i + 1, 0)
+                for b in range(4):
+                    flip(i + 1, b)
+                for b in range(2):
+                    silu(i + 1, b)
+                    gain(i + 1, b)
             product(k, 1)
-            finish(k - 1, *tiles[1])
             if more and ends:
-                flip(i + 1, 3)
-                silu(i + 1, 1)
-                gain(i + 1, 1)
+                invert(i + 1)
+            finish(k - 1, *tiles[1])
             quantise(k)
             finish(k - 1, *tiles[2])
             if more and ends:
-                invert(i + 1)
                 spread_inv(i + 1)
             for t in tiles[:3]:
                 matmuls(k, *t)
             if more and ends:
-                silu(i + 1, 2)
-                gain(i + 1, 2)
-                silu(i + 1, 3)
-                gain(i + 1, 3)
+                for b in range(2, 4):
+                    silu(i + 1, b)
+                    gain(i + 1, b)
             finish(k - 1, *tiles[3])
         last = UNITS - 1
         finish(last, *tiles[0])

@@ -25,8 +25,8 @@ OUT_HALVES = OUTF // BANK
 UNIT = 2
 WIDTH = UNIT * P
 UNITS = TOKENS // WIDTH
-GROUPS = ((0,), (1,), (2, 3), (4, 5), (6, 7))
-SCALAR_OUT = ()
+GROUPS = ((0,), (1,), (2,), (3,), (4, 5), (6, 7))
+SCALAR_OUT = ((5,0,1), (5,1,1), (6,0,1), (6,1,1), )
 
 FLOPS = 2 * TOKENS * FEAT * OUTF
 
@@ -59,10 +59,9 @@ def tile_normlocalattention_pb_kernel(tc, attn_out, norm_scale, norm_gate, w_o, 
 
         x_tiles = [keep.tile([P, FEAT], BF16, name="x%d" % i) for i in range(TOKENS // P)]
         w_tiles = [keep.tile([P, FEAT], BF16, name="w%d" % i) for i in range(OUTF // P)]
-        bias_row = keep.tile([P, OUTF], BF16)
+        bias = keep.tile([P, OUTF], BF16)
         ident = keep.tile([P, P], F32)
         make_identity(nc, ident[:])
-        nc.gpsimd.memset(bias_row[:], 0.0)
 
         def load_x(first, last):
             for i in range(first, last):
@@ -71,18 +70,10 @@ def tile_normlocalattention_pb_kernel(tc, attn_out, norm_scale, norm_gate, w_o, 
         load_x(0, 4)
         for i in range(OUTF // P):
             nc.sync.dma_start(out=w_tiles[i][:], in_=w_o[i * P : (i + 1) * P, :])
-        nc.sync.dma_start(out=bias_row[0:1, :], in_=b_o.rearrange("(r c) -> r c", r=1))
-        load_x(4, TOKENS // P)
+        load_x(4, 8)
+        nc.sync.dma_start(out=bias[:], in_=b_o.partition_broadcast(P))
+        load_x(8, TOKENS // P)
 
-        ones = keep.tile([P, P], BF16)
-        nc.vector.memset(ones[:], 1.0)
-        warm_in = keep.tile([P, P], F32)
-        nc.vector.memset(warm_in[:], 0.0)
-        warm_ps = sums.tile([P, P], F32, name="warm_ps", tag="sum")
-
-        def keep_warm(n):
-            for r in range(n):
-                nc.tensor.matmul(out=warm_ps[:], lhsT=warm_in[:], rhs=warm_in[:], start=True, stop=True)
         halves_exp = keep.tile([P, 2 * UNIT], F32)
         nc.vector.memset(halves_exp[:], 0.5)
 
@@ -153,9 +144,12 @@ def tile_normlocalattention_pb_kernel(tc, attn_out, norm_scale, norm_gate, w_o, 
                     op1=ALU.add,
                 )
 
-        def square(i, on_vector=()):
-            mean_sq[i] = small.tile([P, 2 * UNIT], F32, name="mean_sq")
+        def square(i, on_vector=(), part=range(4)):
+            if 0 in part:
+                mean_sq[i] = small.tile([P, 2 * UNIT], F32, name="mean_sq")
             for j, t in enumerate(tiles_of(i)):
+                if j not in part:
+                    continue
                 squares = small.tile([P, FEAT], BF16, name="squares")
                 if t in on_vector:
                     nc.vector.scalar_tensor_tensor(
@@ -272,49 +266,40 @@ def tile_normlocalattention_pb_kernel(tc, attn_out, norm_scale, norm_gate, w_o, 
                     out=w_codes[:, g, cols].bitcast(FP8X4), scales=w_scales[:, g, cols], in_=w_grouped[g, h][:]
                 )
 
-        bias = keep.tile([P, OUTF], F32)
-
-        def spread_bias(engine_copy):
-            for h in range(OUT_HALVES):
-                cols = slice(h * BANK, (h + 1) * BANK)
-                bias_ps = sums.tile([P, BANK], F32, name="bias_ps", tag="sum")
-                nc.tensor.matmul(out=bias_ps[:], lhsT=ones[:], rhs=bias_row[:, cols], start=True, stop=True)
-                engine_copy(out=bias[:, cols], in_=bias_ps[:])
-
         tiles = [(j, h) for j in range(UNIT) for h in range(OUT_HALVES)]
         square(0, on_vector=(0, 1))
-        root(0)
         flip(0, 0)
         flip(0, 1)
         silu(0, 0)
         gain(0, 0)
+        root(0)
         silu(0, 1)
         gain(0, 1)
-        square(1, on_vector=(2, 3))
+        square(1)
         root(1)
+        group_w(0, 0, 0, nc.vector.tensor_copy)
+        group_w(0, 0, 1, nc.vector.tensor_copy)
+        invert(0)
         flip(1, 0)
         flip(1, 1)
+        spread_inv(0)
         silu(1, 0)
         gain(1, 0)
         silu(1, 1)
         gain(1, 1)
-        invert(0)
-        for g in range(PASSES):
-            for fp in range(2):
-                group_w(0, g, fp, nc.vector.tensor_copy)
-        spread_inv(0)
-        square(2)
-        root(2)
+        group_w(0, 1, 0, nc.vector.tensor_copy)
+        product(0, 0)
+        group_w(0, 1, 1, nc.vector.tensor_copy)
+        product(0, 1)
         for g in range(PASSES):
             for fp in range(2):
                 group_w(1, g, fp, nc.scalar.copy)
-        product(0, 0)
-        product(0, 1)
-        invert(1)
-        spread_bias(nc.scalar.copy)
-        spread_inv(1)
         quantise_w(0)
+        invert(1)
         quantise(0)
+        spread_inv(1)
+        square(2)
+        root(2)
         flip(2, 0)
         flip(2, 1)
         silu(2, 0)
@@ -322,57 +307,41 @@ def tile_normlocalattention_pb_kernel(tc, attn_out, norm_scale, norm_gate, w_o, 
         silu(2, 1)
         gain(2, 1)
         quantise_w(1)
-        product(1, 0)
         for t in tiles[:3]:
             matmuls(0, *t)
-        finish(0, *tiles[0])
-        matmuls(0, *tiles[3])
-        flip(2, 2)
-        flip(2, 3)
-        silu(2, 2)
-        gain(2, 2)
-        silu(2, 3)
-        gain(2, 3)
-        product(1, 1)
-        finish(0, *tiles[1])
-        invert(2)
-        quantise(1)
-        finish(0, *tiles[2])
-        spread_inv(2)
-        for t in tiles[:3]:
-            matmuls(1, *t)
-        finish(0, *tiles[3])
 
-        for k in range(2, UNITS):
-            i = group_of[k]
-            begins, ends = k == GROUPS[i][0], k == GROUPS[i][-1]
-            more = i + 1 < len(GROUPS)
-            if more and begins:
-                square(i + 1)
-                root(i + 1)
+        half = {1: (3, (0, 1), 0), 2: (4, (0, 1, 2, 3), 1), 3: (4, (0, 1, 2, 3), 2), 4: (5, (0, 1, 2, 3), 1), 5: (5, (0, 1, 2, 3), 2)}
+        for k in range(1, UNITS):
+            n, banks, part = half.get(k, (0, (), 0))
+            if part in (0, 1) and n:
+                square(n)
+                root(n)
             product(k, 0)
             finish(k - 1, *tiles[0])
             matmuls(k - 1, *tiles[3])
-            if more and begins:
-                for b in range(4):
-                    flip(i + 1, b)
-                for b in range(2):
-                    silu(i + 1, b)
-                    gain(i + 1, b)
+            if part in (0, 1):
+                for b in banks:
+                    flip(n, b)
+            first = banks if part == 0 else (banks[:2] if part == 1 else banks[2:])
+            if part in (0, 1):
+                for b in first:
+                    silu(n, b)
+                    gain(n, b)
             product(k, 1)
-            if more and ends:
-                invert(i + 1)
+            m = group_of[k] + 1
+            if k == GROUPS[group_of[k]][-1] and m < len(GROUPS):
+                invert(m)
             finish(k - 1, *tiles[1])
             quantise(k)
             finish(k - 1, *tiles[2])
-            if more and ends:
-                spread_inv(i + 1)
+            if k == GROUPS[group_of[k]][-1] and m < len(GROUPS):
+                spread_inv(m)
             for t in tiles[:3]:
                 matmuls(k, *t)
-            if more and ends:
-                for b in range(2, 4):
-                    silu(i + 1, b)
-                    gain(i + 1, b)
+            if part == 2:
+                for b in first:
+                    silu(n, b)
+                    gain(n, b)
             finish(k - 1, *tiles[3])
         last = UNITS - 1
         finish(last, *tiles[0])

@@ -19,6 +19,7 @@ EPS = 1e-8
 PACK = 4
 PASSES = FEAT // (P * PACK)
 PAIR = 2
+GATE_SHIFT = 1.0001e-20
 PLANES = FEAT // P
 BANK = 512
 OUT_HALVES = OUTF // BANK
@@ -26,7 +27,8 @@ UNIT = 2
 WIDTH = UNIT * P
 UNITS = TOKENS // WIDTH
 GROUPS = ((0,), (1,), (2,), (3,), (4, 5), (6, 7))
-SCALAR_OUT = ((5,0,1), (5,1,1), (6,0,1), (6,1,1), )
+SCALAR_GAIN = ((5, 1), (5, 3), (5, 5), (5, 7), )
+SCALAR_OUT = ((5,0,1), (5,1,1), (6,0,1), (6,1,1), (4,1,1), )
 
 FLOPS = 2 * TOKENS * FEAT * OUTF
 
@@ -67,7 +69,11 @@ def tile_normlocalattention_pb_kernel(tc, attn_out, norm_scale, norm_gate, w_o, 
             for i in range(first, last):
                 nc.sync.dma_start(out=x_tiles[i][:], in_=x_rows[i * P : (i + 1) * P, :])
 
-        load_x(0, 4)
+        for g in range(PASSES):
+            feats = slice(g * P * PACK, (g + 1) * P * PACK)
+            for i in range(UNIT):
+                nc.sync.dma_start(out=x_tiles[i][:, feats], in_=x_rows[i * P : (i + 1) * P, feats])
+        load_x(UNIT, 2 * UNIT)
         for i in range(OUTF // P):
             nc.sync.dma_start(out=w_tiles[i][:], in_=w_o[i * P : (i + 1) * P, :])
         load_x(4, 8)
@@ -77,16 +83,8 @@ def tile_normlocalattention_pb_kernel(tc, attn_out, norm_scale, norm_gate, w_o, 
         halves_exp = keep.tile([P, 2 * UNIT], F32)
         nc.vector.memset(halves_exp[:], 0.5)
 
-        gate_abs = keep.tile([P, PLANES], F32)
-        nc.vector.scalar_tensor_tensor(
-            out=gate_abs[:], in0=gate_raw[:], scalar=-1.0, in1=gate_raw[:], op0=ALU.mult, op1=ALU.max
-        )
-        gate_zero = keep.tile([P, PLANES], F32)
-        nc.vector.tensor_scalar(
-            out=gate_zero[:], in0=gate_abs[:], scalar1=1e-20, scalar2=2e-20, op0=ALU.is_lt, op1=ALU.mult
-        )
         gate = keep.tile([P, PLANES], F32)
-        nc.vector.tensor_tensor(out=gate[:], in0=gate_zero[:], in1=gate_raw[:], op=ALU.add)
+        nc.vector.tensor_scalar_add(out=gate[:], in0=gate_raw[:], scalar1=GATE_SHIFT)
         gate_inv = keep.tile([P, PLANES], F32)
         nc.vector.reciprocal(out=gate_inv[:], in_=gate[:])
         ratio = keep.tile([P, PLANES], F32)
@@ -135,6 +133,11 @@ def tile_normlocalattention_pb_kernel(tc, attn_out, norm_scale, norm_gate, w_o, 
         def gain(i, b):
             n = tokens_of(i)
             for c in planes_of(i, b):
+                if (i, c) in SCALAR_GAIN:
+                    nc.scalar.activation(
+                        out=z[i][:, c, 0:n], in_=z[i][:, c, 0:n], func=ACT.Copy, scale=ratio[:, c : c + 1]
+                    )
+                    continue
                 nc.gpsimd.tensor_scalar(
                     out=z[i][:, c, 0:n],
                     in0=z[i][:, c, 0:n],

from contextlib import ExitStack

import concourse.mybir as mybir
from concourse.masks import make_identity

F32 = mybir.dt.float32
BF16 = mybir.dt.bfloat16
U32 = mybir.dt.uint32
U8 = mybir.dt.uint8
FP8X4 = mybir.dt.float8_e4m3fn_x4
ACT = mybir.ActivationFunctionType
ALU = mybir.AluOpType

P = 128
TOKENS = 2048
FEAT = 1024
OUTF = 1024
EPS = 1e-8
PACK = 4
PASSES = FEAT // (P * PACK)
PAIR = 2
GATE_SHIFT = 1.0001e-20
PLANES = FEAT // P
BANK = 512
OUT_HALVES = OUTF // BANK
UNIT = 2
WIDTH = UNIT * P
UNITS = TOKENS // WIDTH
GROUPS = ((0,), (1,), (2,), (3,), (4, 5), (6, 7))
SCALAR_GAIN = ((5, 1), (5, 3), (5, 5), (5, 7), )
SCALAR_OUT = ((5,0,1), (5,1,1), (6,0,1), (6,1,1), (4,1,1), )

FLOPS = 2 * TOKENS * FEAT * OUTF


def tile_normlocalattention_pb_kernel(tc, attn_out, norm_scale, norm_gate, w_o, b_o, out):
    nc = tc.nc
    x_rows = attn_out.rearrange("l n e -> (l n) e")
    out_rows = out.rearrange("l n f -> (l n) f")

    with ExitStack() as stack:
        keep = stack.enter_context(tc.tile_pool(name="keep", bufs=1))
        planes = stack.enter_context(tc.tile_pool(name="planes", bufs=3))
        small = stack.enter_context(tc.tile_pool(name="small", bufs=3))
        results = stack.enter_context(tc.tile_pool(name="results", bufs=4))
        flipped = stack.enter_context(tc.psum_pool(name="flipped", bufs=4))
        spread = stack.enter_context(tc.psum_pool(name="spread", bufs=1))
        sums = stack.enter_context(tc.psum_pool(name="sums", bufs=3))
        stack.enter_context(tc.manual_schedule())

        gate_raw = keep.tile([P, PLANES], BF16)
        scale_raw = keep.tile([P, PLANES], BF16)
        for raw, vec in ((gate_raw, norm_gate), (scale_raw, norm_scale)):
            nc.scalar.dma_start(
                out=raw[:].rearrange("p (g t) -> p g t", t=PACK),
                in_=vec.rearrange("(g p t) -> p g t", g=PASSES, t=PACK),
            )
        warm = keep.tile([P, 1], F32)
        nc.vector.memset(warm[:], 0.0)
        nc.scalar.activation(out=warm[:], in_=warm[:], func=ACT.Silu)

        x_tiles = [keep.tile([P, FEAT], BF16, name="x%d" % i) for i in range(TOKENS // P)]
        w_tiles = [keep.tile([P, FEAT], BF16, name="w%d" % i) for i in range(OUTF // P)]
        bias = keep.tile([P, OUTF], BF16)
        ident = keep.tile([P, P], F32)
        make_identity(nc, ident[:])

        def load_x(first, last):
            for i in range(first, last):
                nc.sync.dma_start(out=x_tiles[i][:], in_=x_rows[i * P : (i + 1) * P, :])

        for g in range(PASSES):
            feats = slice(g * P * PACK, (g + 1) * P * PACK)
            for i in range(UNIT):
                nc.sync.dma_start(out=x_tiles[i][:, feats], in_=x_rows[i * P : (i + 1) * P, feats])
        load_x(UNIT, 2 * UNIT)
        for i in range(OUTF // P):
            nc.sync.dma_start(out=w_tiles[i][:], in_=w_o[i * P : (i + 1) * P, :])
        load_x(4, 8)
        nc.sync.dma_start(out=bias[:], in_=b_o.partition_broadcast(P))
        load_x(8, TOKENS // P)

        halves_exp = keep.tile([P, 2 * UNIT], F32)
        nc.vector.memset(halves_exp[:], 0.5)

        gate = keep.tile([P, PLANES], F32)
        nc.vector.tensor_scalar_add(out=gate[:], in0=gate_raw[:], scalar1=GATE_SHIFT)
        gate_inv = keep.tile([P, PLANES], F32)
        nc.vector.reciprocal(out=gate_inv[:], in_=gate[:])
        ratio = keep.tile([P, PLANES], F32)
        nc.vector.tensor_tensor(out=ratio[:], in0=gate_inv[:], in1=scale_raw[:], op=ALU.mult)

        def word_slice(g, u):
            return slice(g * PAIR * P + u, (g + 1) * PAIR * P, PAIR)

        z, mean_sq, inv, inv_ps, x_flip, y_grouped, y_codes, y_scales, res, acc = ({} for i in range(10))
        group_of = {k: i for i, units in enumerate(GROUPS) for k in units}

        def tokens_of(i):
            return len(GROUPS[i]) * WIDTH

        def tiles_of(i):
            return range(UNIT * GROUPS[i][0], UNIT * (GROUPS[i][-1] + 1))

        def toks_of(k):
            first = (k - GROUPS[group_of[k]][0]) * WIDTH
            return slice(first, first + WIDTH)

        def flip(i, b):
            n = tokens_of(i)
            per_bank = BANK // n
            x_flip[i, b] = flipped.tile([P, per_bank, n], F32, name="x_flip", tag="flip")
            for s in range(per_bank):
                g, u = divmod(b * per_bank + s, PAIR)
                for j, t in enumerate(tiles_of(i)):
                    nc.tensor.transpose(
                        x_flip[i, b][:, s, j * P : (j + 1) * P], x_tiles[t][:].bitcast(F32)[:, word_slice(g, u)], ident[:]
                    )

        def planes_of(i, b):
            per_bank = BANK // tokens_of(i)
            return range(PAIR * per_bank * b, PAIR * per_bank * (b + 1))

        def silu(i, b):
            if b == 0:
                z[i] = planes.tile([P, PLANES, BANK], F32, name="z")
            n = tokens_of(i)
            for c in planes_of(i, b):
                s, e = divmod(c - planes_of(i, b)[0], PAIR)
                half = x_flip[i, b][:, s, :].bitcast(BF16).rearrange("p (n e) -> p n e", e=PAIR)[:, :, e]
                nc.scalar.activation(out=z[i][:, c, 0:n], in_=half, func=ACT.Silu, scale=gate[:, c : c + 1])

        def gain(i, b):
            n = tokens_of(i)
            for c in planes_of(i, b):
                if (i, c) in SCALAR_GAIN:
                    nc.scalar.activation(
                        out=z[i][:, c, 0:n], in_=z[i][:, c, 0:n], func=ACT.Copy, scale=ratio[:, c : c + 1]
                    )
                    continue
                nc.gpsimd.tensor_scalar(
                    out=z[i][:, c, 0:n],
                    in0=z[i][:, c, 0:n],
                    scalar1=ratio[:, c : c + 1],
                    scalar2=0.0,
                    op0=ALU.mult,
                    op1=ALU.add,
                )

        def square(i, on_vector=(), part=range(4)):
            if 0 in part:
                mean_sq[i] = small.tile([P, 2 * UNIT], F32, name="mean_sq")
            for j, t in enumerate(tiles_of(i)):
                if j not in part:
                    continue
                squares = small.tile([P, FEAT], BF16, name="squares")
                if t in on_vector:
                    nc.vector.scalar_tensor_tensor(
                        out=squares[:],
                        in0=x_tiles[t][:],
                        scalar=1.0 / FEAT,
                        in1=x_tiles[t][:],
                        op0=ALU.mult,
                        op1=ALU.mult,
                        accum_out=mean_sq[i][:, j : j + 1],
                    )
                else:
                    nc.scalar.activation(
                        out=squares[:],
                        in_=x_tiles[t][:],
                        func=ACT.Square,
                        scale=1.0 / 32.0,
                        accum_out=mean_sq[i][:, j : j + 1],
                    )

        def root(i):
            m = len(tiles_of(i))
            inv[i] = small.tile([P, 2 * UNIT], F32, name="inv")
            nc.gpsimd.tensor_tensor(out=inv[i][:, 0:m], in0=mean_sq[i][:, 0:m], in1=halves_exp[:, 0:m], op=ALU.pow)

        def invert(i):
            m = len(tiles_of(i))
            nc.vector.tensor_scalar_add(out=inv[i][:, 0:m], in0=inv[i][:, 0:m], scalar1=EPS)
            nc.vector.reciprocal(out=inv[i][:, 0:m], in_=inv[i][:, 0:m])

        def spread_inv(i):
            inv_ps[i] = spread.tile([P, BANK], F32, name="inv_ps")
            for j in range(len(tiles_of(i))):
                nc.tensor.transpose(
                    inv_ps[i][:, j * P : (j + 1) * P], inv[i][:, j : j + 1].to_broadcast([P, P]), ident[:]
                )

        def product(k, g):
            if k not in y_grouped:
                y_grouped[k] = small.tile([P, PASSES, WIDTH, PACK], BF16, name="y_grouped", align_bytes=64)
            i, toks = group_of[k], toks_of(k)
            nc.vector.tensor_tensor(
                out=y_grouped[k][:, g].rearrange("p (c i) t -> p c t i", i=PACK),
                in0=z[i][:, g * PACK : (g + 1) * PACK, toks].rearrange("p t (c i) -> p c t i", i=PACK),
                in1=inv_ps[i][:, toks]
                .rearrange("p (c i) -> p c i", i=PACK)
                .unsqueeze(2)
                .to_broadcast([P, WIDTH // PACK, PACK, PACK]),
                op=ALU.mult,
            )

        def quantise(k):
            y_codes[k] = small.tile([P, PASSES, WIDTH], U32, name="y_codes", align_bytes=64)
            y_scales[k] = small.tile([P, PASSES, WIDTH], U8, name="y_scales", align_bytes=64)
            nc.vector.quantize_mx(
                out=y_codes[k][:].rearrange("p g n -> p (g n)").bitcast(FP8X4),
                scales=y_scales[k][:].rearrange("p g n -> p (g n)"),
                in_=y_grouped[k][:].rearrange("p g n t -> p (g n t)"),
            )

        def matmuls(k, j, h):
            acc[k, j, h] = sums.tile([P, BANK], F32, name="acc", tag="sum")
            toks = slice(j * P, (j + 1) * P)
            cols = slice(h * BANK, (h + 1) * BANK)
            for g in range(PASSES):
                nc.tensor.matmul_mx(
                    out=acc[k, j, h][:],
                    lhsT=y_codes[k][:, g, toks].bitcast(FP8X4),
                    lhsT_scale=y_scales[k][:, g, toks],
                    rhs=w_codes[:, g, cols].bitcast(FP8X4),
                    rhs_scale=w_scales[:, g, cols],
                    start=(g == 0),
                    stop=(g == PASSES - 1),
                )

        def finish(k, j, h):
            if h == 0:
                res[k, j] = results.tile([P, OUTF], F32, name="res")
            cols = slice(h * BANK, (h + 1) * BANK)
            if (k, j, h) in SCALAR_OUT:
                part = results.tile([P, BANK], F32, name="part")
                nc.scalar.copy(out=part[:], in_=acc[k, j, h][:])
                nc.gpsimd.tensor_tensor(out=res[k, j][:, cols], in0=part[:], in1=bias[:, cols], op=ALU.add)
            else:
                nc.vector.tensor_tensor(out=res[k, j][:, cols], in0=acc[k, j, h][:], in1=bias[:, cols], op=ALU.add)
            row0 = (UNIT * k + j) * P
            if k == UNITS - 1:
                nc.sync.dma_start(out=out_rows[row0 : row0 + P, cols], in_=res[k, j][:, cols])
            elif h == OUT_HALVES - 1:
                nc.sync.dma_start(out=out_rows[row0 : row0 + P, :], in_=res[k, j][:])

        w_codes = keep.tile([P, PASSES, OUTF], U32, align_bytes=64)
        w_scales = keep.tile([P, PASSES, OUTF], U8, align_bytes=64)
        w_grouped = {}

        def group_w(h, g, fp, engine_copy):
            if fp == 0:
                w_grouped[g, h] = keep.tile([P, BANK * PACK], BF16, name="w_grouped%d%d" % (g, h), align_bytes=64)
            w_words = w_grouped[g, h][:].bitcast(F32).rearrange("p (f u) -> p f u", u=PAIR)
            w_t = flipped.tile([P, PAIR, 2 * P], F32, name="w_t", tag="flip")
            for u in range(PAIR):
                for o in range(2):
                    nc.tensor.transpose(
                        w_t[:, u, o * P : (o + 1) * P],
                        w_tiles[4 * h + 2 * fp + o][:].bitcast(F32)[:, word_slice(g, u)],
                        ident[:],
                    )
            engine_copy(out=w_words[:, fp * 2 * P : (fp + 1) * 2 * P, :], in_=w_t[:].rearrange("p u f -> p f u"))

        def quantise_w(h):
            cols = slice(h * BANK, (h + 1) * BANK)
            for g in range(PASSES):
                nc.vector.quantize_mx(
                    out=w_codes[:, g, cols].bitcast(FP8X4), scales=w_scales[:, g, cols], in_=w_grouped[g, h][:]
                )

        tiles = [(j, h) for j in range(UNIT) for h in range(OUT_HALVES)]
        square(0, on_vector=(0, 1))
        flip(0, 0)
        flip(0, 1)
        silu(0, 0)
        gain(0, 0)
        root(0)
        silu(0, 1)
        gain(0, 1)
        square(1)
        root(1)
        group_w(0, 0, 0, nc.vector.tensor_copy)
        group_w(0, 0, 1, nc.vector.tensor_copy)
        invert(0)
        flip(1, 0)
        flip(1, 1)
        spread_inv(0)
        silu(1, 0)
        gain(1, 0)
        silu(1, 1)
        gain(1, 1)
        group_w(0, 1, 0, nc.vector.tensor_copy)
        product(0, 0)
        group_w(0, 1, 1, nc.vector.tensor_copy)
        product(0, 1)
        for g in range(PASSES):
            for fp in range(2):
                group_w(1, g, fp, nc.scalar.copy)
        quantise_w(0)
        invert(1)
        quantise(0)
        spread_inv(1)
        square(2)
        root(2)
        flip(2, 0)
        flip(2, 1)
        silu(2, 0)
        gain(2, 0)
        silu(2, 1)
        gain(2, 1)
        quantise_w(1)
        for t in tiles[:3]:
            matmuls(0, *t)

        half = {1: (3, (0, 1), 0), 2: (4, (0, 1, 2, 3), 1), 3: (4, (0, 1, 2, 3), 2), 4: (5, (0, 1, 2, 3), 1), 5: (5, (0, 1, 2, 3), 2)}
        for k in range(1, UNITS):
            n, banks, part = half.get(k, (0, (), 0))
            if part in (0, 1) and n:
                square(n)
                root(n)
            product(k, 0)
            finish(k - 1, *tiles[0])
            matmuls(k - 1, *tiles[3])
            if part in (0, 1):
                for b in banks:
                    flip(n, b)
            first = banks if part == 0 else (banks[:2] if part == 1 else banks[2:])
            if part in (0, 1):
                for b in first:
                    silu(n, b)
                    gain(n, b)
            product(k, 1)
            m = group_of[k] + 1
            if k == GROUPS[group_of[k]][-1] and m < len(GROUPS):
                invert(m)
            finish(k - 1, *tiles[1])
            quantise(k)
            finish(k - 1, *tiles[2])
            if k == GROUPS[group_of[k]][-1] and m < len(GROUPS):
                spread_inv(m)
            for t in tiles[:3]:
                matmuls(k, *t)
            if part == 2:
                for b in first:
                    silu(n, b)
                    gain(n, b)
            finish(k - 1, *tiles[3])
        last = UNITS - 1
        finish(last, *tiles[0])
        matmuls(last, *tiles[3])
        for t in tiles[1:]:
            finish(last, *t)
